import numpy as np
import ml_dtypes


def mxq(x, axis, fmt="e4m3"):
    dtype, down = {"e4m3": (ml_dtypes.float8_e4m3fn, 7), "e5m2": (ml_dtypes.float8_e5m2, 14)}[fmt]
    v = np.moveaxis(np.asarray(x, np.float32).astype(ml_dtypes.bfloat16).astype(np.float64), axis, -1)
    blocks = v.reshape(v.shape[:-1] + (-1, 32))
    amax = np.abs(blocks).max(-1, keepdims=True)
    byte = np.maximum(np.where(amax > 0, np.frexp(amax)[1] - 1 + 127, 0) - down, 1)
    scale = np.exp2(byte - 127.0)
    codes = (blocks / scale).astype(np.float32).astype(dtype).astype(np.float64)
    return np.moveaxis((codes * scale).reshape(v.shape), -1, axis)


WIDE = False


def mx_kscale(k):
    if not WIDE:
        return np.ones(k)
    levels = np.array([10, -10, 5, -5, 0])
    a = np.random.permutation(np.resize(levels, k // 512 * 4)).reshape(k // 512, 4)
    idx = np.arange(k)
    return np.exp2(a[idx // 512, idx % 128 // 32])


BF16 = ml_dtypes.bfloat16


def bf(x):
    return np.asarray(x, np.float32).astype(BF16)


def f64(x):
    return np.asarray(x).astype(np.float64)


B, S, M, D, H = 8, 128, 16, 256, 1024


def setup_inputs():
    s = mx_kscale(2 * D)
    lens = np.random.randint(0, M + 1, (B, S))
    valid = (np.arange(M)[None, None, :] < lens[:, :, None]).astype(np.float64)
    src = np.random.standard_normal((B, S, M, D)) / np.sqrt(M) * s[:D]
    neigh = np.random.standard_normal((B, S, M, D)) * 2.0 * valid[..., None] * s[D:]
    return {"src_node_features": bf(src), "neigh_node_features": bf(neigh),
            "W_map": bf(np.random.standard_normal((2 * D, H)) / np.sqrt(2 * D) / s[:, None]),
            "b_map": bf(-0.5 + 0.3 * np.random.standard_normal(H))}


def reference(src_node_features, neigh_node_features, W_map, b_map):
    src, neigh = f64(src_node_features), f64(neigh_node_features)
    valid = np.any(neigh != 0, axis=-1)
    num = np.sum(valid, axis=-1).astype(np.float64)
    neigh_mean = neigh.sum(axis=2) / np.maximum(num, 1.0)[..., None]
    hidden = np.concatenate([src.sum(axis=2), neigh_mean], axis=-1)
    hidden = hidden.reshape(-1, hidden.shape[-1])
    v = (mxq(hidden, 1, "e4m3") @ mxq(f64(W_map), 0, "e4m3")) + f64(b_map)
    return np.where(v >= 0, v, 0.01 * v)

@@ -1,0 +1,146 @@
+from contextlib import ExitStack
+
+import concourse.mybir as mybir
+from concourse.masks import make_identity
+
+F32 = mybir.dt.float32
+BF16 = mybir.dt.bfloat16
+U32 = mybir.dt.uint32
+U8 = mybir.dt.uint8
+FP8X4 = mybir.dt.float8_e4m3fn_x4
+ALU = mybir.AluOpType
+ACT = mybir.ActivationFunctionType
+AXIS = mybir.AxisListType
+
+P = 128
+PACK = 4
+BATCH, NODES, SLOTS, FEAT, HID = 8, 128, 16, 256, 1024
+GROUP_NODES = P // SLOTS
+GROUPS = NODES // GROUP_NODES
+FEAT_HALVES = FEAT // P
+N_TILE = 512
+SLOPE = 0.01
+
+FLOPS = 2 * BATCH * NODES * 2 * FEAT * HID
+
+
+def tile_syntacticgcn_kernel(tc, src, neigh, w_map, b_map, out):
+    nc = tc.nc
+    with ExitStack() as ctx:
+        const = ctx.enter_context(tc.tile_pool(name="const", bufs=1))
+        loads = ctx.enter_context(tc.tile_pool(name="loads", bufs=3))
+        work = ctx.enter_context(tc.tile_pool(name="work", bufs=2))
+        results = ctx.enter_context(tc.tile_pool(name="results", bufs=3))
+        psum_hidden = ctx.enter_context(tc.psum_pool(name="psum_hidden", bufs=2))
+        psum_out = ctx.enter_context(tc.psum_pool(name="psum_out", bufs=4))
+
+        w_raw = const.tile([P, PACK, HID], BF16)
+        nc.sync.dma_start(out=w_raw[:], in_=w_map.rearrange("(t p) n -> p t n", p=P))
+        bias_bf16 = const.tile([P, HID], BF16)
+        nc.scalar.dma_start(out=bias_bf16[:], in_=b_map.partition_broadcast(P))
+
+        identity = const.tile([P, P], F32)
+        make_identity(nc, identity[:])
+        select_f32 = const.tile([P, GROUP_NODES], F32)
+        nc.vector.tensor_reduce(
+            out=select_f32[:],
+            in_=identity[:].rearrange("p (j s) -> p j s", s=SLOTS),
+            axis=AXIS.X,
+            op=ALU.add,
+        )
+        select = const.tile([P, GROUP_NODES], BF16)
+        nc.vector.tensor_copy(out=select[:], in_=select_f32[:])
+
+        w_grouped = const.tile([P, HID, PACK], BF16, align_bytes=64)
+        w_codes = const.tile([P, HID], U32, align_bytes=64)
+        w_scales = const.tile([P, HID], U8, align_bytes=64)
+        nc.vector.tensor_copy(out=w_grouped[:], in_=w_raw[:].rearrange("p t n -> p n t"))
+        nc.vector.quantize_mx(
+            out=w_codes[:].bitcast(FP8X4),
+            scales=w_scales[:],
+            in_=w_grouped[:].rearrange("p n t -> p (n t)"),
+        )
+        bias = const.tile([P, HID], F32)
+        nc.vector.tensor_copy(out=bias[:], in_=bias_bf16[:])
+
+        for b in range(BATCH):
+            src_t = loads.tile([P, GROUPS, FEAT], BF16)
+            nc.sync.dma_start(
+                out=src_t[:], in_=src[b].rearrange("(g j) s f -> (j s) g f", j=GROUP_NODES)
+            )
+            neigh_t = loads.tile([P, SLOTS, FEAT], BF16)
+            nc.sync.dma_start(out=neigh_t[:], in_=neigh[b])
+
+            hidden_t = psum_hidden.tile([P, PACK, NODES], F32)
+            for g in range(GROUPS):
+                for h in range(FEAT_HALVES):
+                    nc.tensor.matmul(
+                        out=hidden_t[:, h, g * GROUP_NODES : (g + 1) * GROUP_NODES],
+                        lhsT=src_t[:, g, h * P : (h + 1) * P],
+                        rhs=select[:],
+                        start=True,
+                        stop=True,
+                    )
+
+            abs_values = work.tile([P, SLOTS, FEAT], BF16)
+            abs_sum = work.tile([P, SLOTS], F32)
+            for s in range(SLOTS):
+                nc.scalar.activation(
+                    out=abs_values[:, s, :],
+                    in_=neigh_t[:, s, :],
+                    func=ACT.Abs,
+                    accum_out=abs_sum[:, s : s + 1],
+                )
+            valid = work.tile([P, SLOTS], F32)
+            nc.vector.tensor_single_scalar(out=valid[:], in_=abs_sum[:], scalar=0.0, op=ALU.is_gt)
+            num = work.tile([P, 1], F32)
+            nc.vector.tensor_reduce(out=num[:], in_=valid[:], axis=AXIS.X, op=ALU.add)
+            num_floor = work.tile([P, 1], F32)
+            nc.vector.tensor_scalar_max(out=num_floor[:], in0=num[:], scalar1=1.0)
+            inv_num = work.tile([P, 1], F32)
+            nc.vector.reciprocal(out=inv_num[:], in_=num_floor[:])
+
+            sum8 = work.tile([P, 8, FEAT], F32)
+            nc.vector.tensor_tensor(out=sum8[:], in0=neigh_t[:, 0:8, :], in1=neigh_t[:, 8:16, :], op=ALU.add)
+            sum4 = work.tile([P, 4, FEAT], F32)
+            nc.vector.tensor_tensor(out=sum4[:], in0=sum8[:, 0:4, :], in1=sum8[:, 4:8, :], op=ALU.add)
+            sum2 = work.tile([P, 2, FEAT], F32)
+            nc.vector.tensor_tensor(out=sum2[:], in0=sum4[:, 0:2, :], in1=sum4[:, 2:4, :], op=ALU.add)
+            sum1 = work.tile([P, FEAT], F32)
+            nc.vector.tensor_tensor(out=sum1[:], in0=sum2[:, 0, :], in1=sum2[:, 1, :], op=ALU.add)
+            mean = work.tile([P, FEAT], F32)
+            nc.vector.tensor_scalar_mul(out=mean[:], in0=sum1[:], scalar1=inv_num[:, 0:1])
+
+            for h in range(FEAT_HALVES):
+                nc.tensor.transpose(
+                    hidden_t[:, FEAT_HALVES + h, :], mean[:, h * P : (h + 1) * P], identity[:]
+                )
+
+            grouped = work.tile([P, NODES, PACK], BF16, align_bytes=64)
+            nc.scalar.copy(out=grouped[:], in_=hidden_t[:].rearrange("p t n -> p n t"))
+            h_codes = work.tile([P, NODES], U32, align_bytes=64)
+            h_scales = work.tile([P, NODES], U8, align_bytes=64)
+            nc.vector.quantize_mx(
+                out=h_codes[:].bitcast(FP8X4),
+                scales=h_scales[:],
+                in_=grouped[:].rearrange("p n t -> p (n t)"),
+            )
+
+            result = results.tile([P, HID], F32)
+            for c in range(HID // N_TILE):
+                cols = slice(c * N_TILE, (c + 1) * N_TILE)
+                acc = psum_out.tile([P, N_TILE], F32)
+                nc.tensor.matmul_mx(
+                    out=acc[:],
+                    lhsT=h_codes[:].bitcast(FP8X4),
+                    lhsT_scale=h_scales[:],
+                    rhs=w_codes[:, cols].bitcast(FP8X4),
+                    rhs_scale=w_scales[:, cols],
+                    start=True,
+                    stop=True,
+                )
+                nc.vector.tensor_tensor(out=result[:, cols], in0=acc[:], in1=bias[:, cols], op=ALU.add)
+            nc.vector.scalar_tensor_tensor(
+                out=result[:], in0=result[:], scalar=SLOPE, in1=result[:], op0=ALU.mult, op1=ALU.max
+            )
+            nc.gpsimd.dma_start(out=out[b * NODES : (b + 1) * NODES, :], in_=result[:])

@@ -28,16 +28,30 @@ def tile_syntacticgcn_kernel(tc, src, neigh, w_map, b_map, out):
     nc = tc.nc
     with ExitStack() as ctx:
         const = ctx.enter_context(tc.tile_pool(name="const", bufs=1))
-        loads = ctx.enter_context(tc.tile_pool(name="loads", bufs=3))
+        loads = ctx.enter_context(tc.tile_pool(name="loads", bufs=BATCH))
+        scratch = ctx.enter_context(tc.tile_pool(name="scratch", bufs=1))
         work = ctx.enter_context(tc.tile_pool(name="work", bufs=2))
         results = ctx.enter_context(tc.tile_pool(name="results", bufs=3))
         psum_hidden = ctx.enter_context(tc.psum_pool(name="psum_hidden", bufs=2))
         psum_out = ctx.enter_context(tc.psum_pool(name="psum_out", bufs=4))
 
         w_raw = const.tile([P, PACK, HID], BF16)
-        nc.sync.dma_start(out=w_raw[:], in_=w_map.rearrange("(t p) n -> p t n", p=P))
-        bias_bf16 = const.tile([P, HID], BF16)
-        nc.scalar.dma_start(out=bias_bf16[:], in_=b_map.partition_broadcast(P))
+        bias = const.tile([P, HID], BF16)
+        src_tiles = []
+        neigh_tiles = []
+        for b in range(BATCH):
+            neigh_t = loads.tile([P, SLOTS, FEAT], BF16)
+            nc.sync.dma_start(out=neigh_t[:], in_=neigh[b])
+            neigh_tiles.append(neigh_t)
+            if b == 0:
+                nc.sync.dma_start(out=w_raw[:], in_=w_map.rearrange("(t p) n -> p t n", p=P))
+            src_t = loads.tile([P, GROUPS, FEAT], BF16)
+            nc.sync.dma_start(
+                out=src_t[:], in_=src[b].rearrange("(g j) s f -> (j s) g f", j=GROUP_NODES)
+            )
+            src_tiles.append(src_t)
+            if b == 0:
+                nc.sync.dma_start(out=bias[:], in_=b_map.partition_broadcast(P))
 
         identity = const.tile([P, P], F32)
         make_identity(nc, identity[:])
@@ -60,16 +74,10 @@ def tile_syntacticgcn_kernel(tc, src, neigh, w_map, b_map, out):
             scales=w_scales[:],
             in_=w_grouped[:].rearrange("p n t -> p (n t)"),
         )
-        bias = const.tile([P, HID], F32)
-        nc.vector.tensor_copy(out=bias[:], in_=bias_bf16[:])
 
         for b in range(BATCH):
-            src_t = loads.tile([P, GROUPS, FEAT], BF16)
-            nc.sync.dma_start(
-                out=src_t[:], in_=src[b].rearrange("(g j) s f -> (j s) g f", j=GROUP_NODES)
-            )
-            neigh_t = loads.tile([P, SLOTS, FEAT], BF16)
-            nc.sync.dma_start(out=neigh_t[:], in_=neigh[b])
+            src_t = src_tiles[b]
+            neigh_t = neigh_tiles[b]
 
             hidden_t = psum_hidden.tile([P, PACK, NODES], F32)
             for g in range(GROUPS):
@@ -82,7 +90,7 @@ def tile_syntacticgcn_kernel(tc, src, neigh, w_map, b_map, out):
                         stop=True,
                     )
 
-            abs_values = work.tile([P, SLOTS, FEAT], BF16)
+            abs_values = scratch.tile([P, SLOTS, FEAT], BF16)
             abs_sum = work.tile([P, SLOTS], F32)
             for s in range(SLOTS):
                 nc.scalar.activation(
@@ -92,9 +100,8 @@ def tile_syntacticgcn_kernel(tc, src, neigh, w_map, b_map, out):
                     accum_out=abs_sum[:, s : s + 1],
                 )
             valid = work.tile([P, SLOTS], F32)
-            nc.vector.tensor_single_scalar(out=valid[:], in_=abs_sum[:], scalar=0.0, op=ALU.is_gt)
             num = work.tile([P, 1], F32)
-            nc.vector.tensor_reduce(out=num[:], in_=valid[:], axis=AXIS.X, op=ALU.add)
+            nc.scalar.activation(out=valid[:], in_=abs_sum[:], func=ACT.Sign, accum_out=num[:])
             num_floor = work.tile([P, 1], F32)
             nc.vector.tensor_scalar_max(out=num_floor[:], in0=num[:], scalar1=1.0)
             inv_num = work.tile([P, 1], F32)

@@ -34,24 +34,140 @@ def tile_syntacticgcn_kernel(tc, src, neigh, w_map, b_map, out):
         results = ctx.enter_context(tc.tile_pool(name="results", bufs=3))
         psum_hidden = ctx.enter_context(tc.psum_pool(name="psum_hidden", bufs=2))
         psum_out = ctx.enter_context(tc.psum_pool(name="psum_out", bufs=4))
+        ctx.enter_context(tc.manual_schedule())
 
-        w_raw = const.tile([P, PACK, HID], BF16)
-        bias = const.tile([P, HID], BF16)
-        src_tiles = []
-        neigh_tiles = []
-        for b in range(BATCH):
+        src_tiles = {}
+        neigh_tiles = {}
+        partial = {}
+        nums = {}
+        hidden_banks = {}
+        grouped_tiles = {}
+        acc_banks = {}
+        result_tiles = {}
+
+        def load_neigh(b):
             neigh_t = loads.tile([P, SLOTS, FEAT], BF16)
             nc.sync.dma_start(out=neigh_t[:], in_=neigh[b])
-            neigh_tiles.append(neigh_t)
-            if b == 0:
-                nc.sync.dma_start(out=w_raw[:], in_=w_map.rearrange("(t p) n -> p t n", p=P))
+            neigh_tiles[b] = neigh_t
+
+        def load_src(b):
             src_t = loads.tile([P, GROUPS, FEAT], BF16)
             nc.sync.dma_start(
                 out=src_t[:], in_=src[b].rearrange("(g j) s f -> (j s) g f", j=GROUP_NODES)
             )
-            src_tiles.append(src_t)
-            if b == 0:
-                nc.sync.dma_start(out=bias[:], in_=b_map.partition_broadcast(P))
+            src_tiles[b] = src_t
+
+        def count_slots(b):
+            abs_values = scratch.tile([P, SLOTS, FEAT], BF16)
+            abs_sum = work.tile([P, SLOTS], F32)
+            for s in range(SLOTS):
+                nc.scalar.activation(
+                    out=abs_values[:, s, :],
+                    in_=neigh_tiles[b][:, s, :],
+                    func=ACT.Abs,
+                    accum_out=abs_sum[:, s : s + 1],
+                )
+            valid = work.tile([P, SLOTS], F32)
+            num = work.tile([P, 1], F32)
+            nc.scalar.activation(out=valid[:], in_=abs_sum[:], func=ACT.Sign, accum_out=num[:])
+            nums[b] = num
+
+        def clamp_count(b):
+            num_floor = work.tile([P, 1], F32)
+            nc.vector.tensor_scalar_max(out=num_floor[:], in0=nums[b][:], scalar1=1.0)
+            nums[b] = num_floor
+
+        def invert_count(b):
+            inv_num = work.tile([P, 1], F32)
+            nc.vector.reciprocal(out=inv_num[:], in_=nums[b][:])
+            nums[b] = inv_num
+
+        def halve_slots(b, width):
+            folded = partial.get(b, neigh_tiles[b])
+            halved = work.tile([P, width, FEAT], F32, name="sum%d" % width)
+            nc.vector.tensor_tensor(
+                out=halved[:],
+                in0=folded[:, 0:width, :],
+                in1=folded[:, width : 2 * width, :],
+                op=ALU.add,
+            )
+            partial[b] = halved
+
+        def sum_src(b):
+            hidden_t = psum_hidden.tile([P, PACK, NODES], F32)
+            for g in range(GROUPS):
+                for h in range(FEAT_HALVES):
+                    nc.tensor.matmul(
+                        out=hidden_t[:, h, g * GROUP_NODES : (g + 1) * GROUP_NODES],
+                        lhsT=src_tiles[b][:, g, h * P : (h + 1) * P],
+                        rhs=select[:],
+                        start=True,
+                        stop=True,
+                    )
+            hidden_banks[b] = hidden_t
+
+        def scale_and_transpose(b):
+            mean = work.tile([P, FEAT], F32)
+            nc.vector.tensor_scalar_mul(out=mean[:], in0=partial[b][:, 0, :], scalar1=nums[b][:, 0:1])
+            for h in range(FEAT_HALVES):
+                nc.tensor.transpose(
+                    hidden_banks[b][:, FEAT_HALVES + h, :], mean[:, h * P : (h + 1) * P], identity[:]
+                )
+
+        def group_hidden(b):
+            grouped = work.tile([P, NODES, PACK], BF16, align_bytes=64)
+            nc.scalar.copy(out=grouped[:], in_=hidden_banks[b][:].rearrange("p t n -> p n t"))
+            grouped_tiles[b] = grouped
+
+        def quantise_and_multiply(b):
+            h_codes = work.tile([P, NODES], U32, align_bytes=64)
+            h_scales = work.tile([P, NODES], U8, align_bytes=64)
+            nc.vector.quantize_mx(
+                out=h_codes[:].bitcast(FP8X4),
+                scales=h_scales[:],
+                in_=grouped_tiles[b][:].rearrange("p n t -> p (n t)"),
+            )
+            for c in range(HID // N_TILE):
+                cols = slice(c * N_TILE, (c + 1) * N_TILE)
+                acc = psum_out.tile([P, N_TILE], F32)
+                nc.tensor.matmul_mx(
+                    out=acc[:],
+                    lhsT=h_codes[:].bitcast(FP8X4),
+                    lhsT_scale=h_scales[:],
+                    rhs=w_codes[:, cols].bitcast(FP8X4),
+                    rhs_scale=w_scales[:, cols],
+                    start=True,
+                    stop=True,
+                )
+                acc_banks[(b, c)] = acc
+
+        def add_bias(b, c):
+            if c == 0:
+                result = results.tile([P, HID], F32)
+                result_tiles[b] = result
+            cols = slice(c * N_TILE, (c + 1) * N_TILE)
+            nc.vector.tensor_tensor(
+                out=result_tiles[b][:, cols], in0=acc_banks[(b, c)][:], in1=bias[:, cols], op=ALU.add
+            )
+
+        def leaky_and_store(b):
+            v = result_tiles[b]
+            nc.vector.scalar_tensor_tensor(
+                out=v[:], in0=v[:], scalar=SLOPE, in1=v[:], op0=ALU.mult, op1=ALU.max
+            )
+            nc.gpsimd.dma_start(out=out[b * NODES : (b + 1) * NODES, :], in_=v[:])
+
+        w_raw = const.tile([P, PACK, HID], BF16)
+        bias = const.tile([P, HID], BF16)
+        load_neigh(0)
+        load_neigh(1)
+        nc.sync.dma_start(out=w_raw[:], in_=w_map.rearrange("(t p) n -> p t n", p=P))
+        load_src(0)
+        nc.sync.dma_start(out=bias[:], in_=b_map.partition_broadcast(P))
+        for b in range(1, BATCH):
+            if b + 1 < BATCH:
+                load_neigh(b + 1)
+            load_src(b)
 
         identity = const.tile([P, P], F32)
         make_identity(nc, identity[:])
@@ -68,86 +184,39 @@ def tile_syntacticgcn_kernel(tc, src, neigh, w_map, b_map, out):
         w_grouped = const.tile([P, HID, PACK], BF16, align_bytes=64)
         w_codes = const.tile([P, HID], U32, align_bytes=64)
         w_scales = const.tile([P, HID], U8, align_bytes=64)
-        nc.vector.tensor_copy(out=w_grouped[:], in_=w_raw[:].rearrange("p t n -> p n t"))
-        nc.vector.quantize_mx(
-            out=w_codes[:].bitcast(FP8X4),
-            scales=w_scales[:],
-            in_=w_grouped[:].rearrange("p n t -> p (n t)"),
-        )
 
-        for b in range(BATCH):
-            src_t = src_tiles[b]
-            neigh_t = neigh_tiles[b]
-
-            hidden_t = psum_hidden.tile([P, PACK, NODES], F32)
-            for g in range(GROUPS):
-                for h in range(FEAT_HALVES):
-                    nc.tensor.matmul(
-                        out=hidden_t[:, h, g * GROUP_NODES : (g + 1) * GROUP_NODES],
-                        lhsT=src_t[:, g, h * P : (h + 1) * P],
-                        rhs=select[:],
-                        start=True,
-                        stop=True,
-                    )
-
-            abs_values = scratch.tile([P, SLOTS, FEAT], BF16)
-            abs_sum = work.tile([P, SLOTS], F32)
-            for s in range(SLOTS):
-                nc.scalar.activation(
-                    out=abs_values[:, s, :],
-                    in_=neigh_t[:, s, :],
-                    func=ACT.Abs,
-                    accum_out=abs_sum[:, s : s + 1],
+        count_slots(0)
+        for b in range(BATCH + 1):
+            sums = b < BATCH
+            finishes = b > 0
+            if b + 1 < BATCH:
+                count_slots(b + 1)
+            if sums:
+                halve_slots(b, 8)
+            if finishes:
+                quantise_and_multiply(b - 1)
+            if sums:
+                sum_src(b)
+                clamp_count(b)
+                halve_slots(b, 4)
+            if finishes:
+                add_bias(b - 1, 0)
+            if sums:
+                invert_count(b)
+                halve_slots(b, 2)
+            if finishes:
+                add_bias(b - 1, 1)
+            if sums:
+                halve_slots(b, 1)
+            if finishes:
+                leaky_and_store(b - 1)
+            if b == 0:
+                nc.vector.tensor_copy(out=w_grouped[:], in_=w_raw[:].rearrange("p t n -> p n t"))
+                nc.vector.quantize_mx(
+                    out=w_codes[:].bitcast(FP8X4),
+                    scales=w_scales[:],
+                    in_=w_grouped[:].rearrange("p n t -> p (n t)"),
                 )
-            valid = work.tile([P, SLOTS], F32)
-            num = work.tile([P, 1], F32)
-            nc.scalar.activation(out=valid[:], in_=abs_sum[:], func=ACT.Sign, accum_out=num[:])
-            num_floor = work.tile([P, 1], F32)
-            nc.vector.tensor_scalar_max(out=num_floor[:], in0=num[:], scalar1=1.0)
-            inv_num = work.tile([P, 1], F32)
-            nc.vector.reciprocal(out=inv_num[:], in_=num_floor[:])
-
-            sum8 = work.tile([P, 8, FEAT], F32)
-            nc.vector.tensor_tensor(out=sum8[:], in0=neigh_t[:, 0:8, :], in1=neigh_t[:, 8:16, :], op=ALU.add)
-            sum4 = work.tile([P, 4, FEAT], F32)
-            nc.vector.tensor_tensor(out=sum4[:], in0=sum8[:, 0:4, :], in1=sum8[:, 4:8, :], op=ALU.add)
-            sum2 = work.tile([P, 2, FEAT], F32)
-            nc.vector.tensor_tensor(out=sum2[:], in0=sum4[:, 0:2, :], in1=sum4[:, 2:4, :], op=ALU.add)
-            sum1 = work.tile([P, FEAT], F32)
-            nc.vector.tensor_tensor(out=sum1[:], in0=sum2[:, 0, :], in1=sum2[:, 1, :], op=ALU.add)
-            mean = work.tile([P, FEAT], F32)
-            nc.vector.tensor_scalar_mul(out=mean[:], in0=sum1[:], scalar1=inv_num[:, 0:1])
-
-            for h in range(FEAT_HALVES):
-                nc.tensor.transpose(
-                    hidden_t[:, FEAT_HALVES + h, :], mean[:, h * P : (h + 1) * P], identity[:]
-                )
-
-            grouped = work.tile([P, NODES, PACK], BF16, align_bytes=64)
-            nc.scalar.copy(out=grouped[:], in_=hidden_t[:].rearrange("p t n -> p n t"))
-            h_codes = work.tile([P, NODES], U32, align_bytes=64)
-            h_scales = work.tile([P, NODES], U8, align_bytes=64)
-            nc.vector.quantize_mx(
-                out=h_codes[:].bitcast(FP8X4),
-                scales=h_scales[:],
-                in_=grouped[:].rearrange("p n t -> p (n t)"),
-            )
-
-            result = results.tile([P, HID], F32)
-            for c in range(HID // N_TILE):
-                cols = slice(c * N_TILE, (c + 1) * N_TILE)
-                acc = psum_out.tile([P, N_TILE], F32)
-                nc.tensor.matmul_mx(
-                    out=acc[:],
-                    lhsT=h_codes[:].bitcast(FP8X4),
-                    lhsT_scale=h_scales[:],
-                    rhs=w_codes[:, cols].bitcast(FP8X4),
-                    rhs_scale=w_scales[:, cols],
-                    start=True,
-                    stop=True,
-                )
-                nc.vector.tensor_tensor(out=result[:, cols], in0=acc[:], in1=bias[:, cols], op=ALU.add)
-            nc.vector.scalar_tensor_tensor(
-                out=result[:], in0=result[:], scalar=SLOPE, in1=result[:], op0=ALU.mult, op1=ALU.max
-            )
-            nc.gpsimd.dma_start(out=out[b * NODES : (b + 1) * NODES, :], in_=result[:])
+            if sums:
+                scale_and_transpose(b)
+                group_hidden(b)

@@ -52,9 +52,10 @@ def tile_syntacticgcn_kernel(tc, src, neigh, w_map, b_map, out):
 
         def load_src(b):
             src_t = loads.tile([P, GROUPS, FEAT], BF16)
-            nc.sync.dma_start(
-                out=src_t[:], in_=src[b].rearrange("(g j) s f -> (j s) g f", j=GROUP_NODES)
-            )
+            by_group = src[b].rearrange("(g j) s f -> (j s) g f", j=GROUP_NODES)
+            for first in range(0, GROUPS, GROUPS // 2):
+                groups = slice(first, first + GROUPS // 2)
+                nc.sync.dma_start(out=src_t[:, groups, :], in_=by_group[:, groups, :])
             src_tiles[b] = src_t
 
         def count_slots(b):
@@ -185,38 +186,40 @@ def tile_syntacticgcn_kernel(tc, src, neigh, w_map, b_map, out):
         w_codes = const.tile([P, HID], U32, align_bytes=64)
         w_scales = const.tile([P, HID], U8, align_bytes=64)
 
-        count_slots(0)
-        for b in range(BATCH + 1):
-            sums = b < BATCH
-            finishes = b > 0
-            if b + 1 < BATCH:
-                count_slots(b + 1)
-            if sums:
-                halve_slots(b, 8)
+        for m in range(BATCH + 2):
+            folds = m < BATCH
+            scales = 1 <= m <= BATCH
+            finishes = m >= 2
             if finishes:
-                quantise_and_multiply(b - 1)
-            if sums:
-                sum_src(b)
-                clamp_count(b)
-                halve_slots(b, 4)
+                group_hidden(m - 2)
+            if folds:
+                count_slots(m)
+                halve_slots(m, 8)
             if finishes:
-                add_bias(b - 1, 0)
-            if sums:
-                invert_count(b)
-                halve_slots(b, 2)
+                quantise_and_multiply(m - 2)
+            if scales:
+                sum_src(m - 1)
+                clamp_count(m - 1)
+            if folds:
+                halve_slots(m, 4)
             if finishes:
-                add_bias(b - 1, 1)
-            if sums:
-                halve_slots(b, 1)
+                add_bias(m - 2, 0)
+            if scales:
+                invert_count(m - 1)
+            if folds:
+                halve_slots(m, 2)
             if finishes:
-                leaky_and_store(b - 1)
-            if b == 0:
+                add_bias(m - 2, 1)
+            if scales:
+                scale_and_transpose(m - 1)
+            if folds:
+                halve_slots(m, 1)
+            if finishes:
+                leaky_and_store(m - 2)
+            if m == 0:
                 nc.vector.tensor_copy(out=w_grouped[:], in_=w_raw[:].rearrange("p t n -> p n t"))
                 nc.vector.quantize_mx(
                     out=w_codes[:].bitcast(FP8X4),
                     scales=w_scales[:],
                     in_=w_grouped[:].rearrange("p n t -> p (n t)"),
                 )
-            if sums:
-                scale_and_transpose(b)
-                group_hidden(b)

@@ -29,9 +29,9 @@ def tile_syntacticgcn_kernel(tc, src, neigh, w_map, b_map, out):
     with ExitStack() as ctx:
         const = ctx.enter_context(tc.tile_pool(name="const", bufs=1))
         loads = ctx.enter_context(tc.tile_pool(name="loads", bufs=BATCH))
+        results = ctx.enter_context(tc.tile_pool(name="results", bufs=BATCH))
         scratch = ctx.enter_context(tc.tile_pool(name="scratch", bufs=1))
         work = ctx.enter_context(tc.tile_pool(name="work", bufs=2))
-        results = ctx.enter_context(tc.tile_pool(name="results", bufs=3))
         psum_hidden = ctx.enter_context(tc.psum_pool(name="psum_hidden", bufs=2))
         psum_out = ctx.enter_context(tc.psum_pool(name="psum_out", bufs=4))
         ctx.enter_context(tc.manual_schedule())
@@ -85,7 +85,8 @@ def tile_syntacticgcn_kernel(tc, src, neigh, w_map, b_map, out):
 
         def halve_slots(b, width):
             folded = partial.get(b, neigh_tiles[b])
-            halved = work.tile([P, width, FEAT], F32, name="sum%d" % width)
+            pool = work if width == 1 else scratch
+            halved = pool.tile([P, width, FEAT], F32, name="sum%d" % width)
             nc.vector.tensor_tensor(
                 out=halved[:],
                 in0=folded[:, 0:width, :],
@@ -156,13 +157,16 @@ def tile_syntacticgcn_kernel(tc, src, neigh, w_map, b_map, out):
             nc.vector.scalar_tensor_tensor(
                 out=v[:], in0=v[:], scalar=SLOPE, in1=v[:], op0=ALU.mult, op1=ALU.max
             )
-            nc.gpsimd.dma_start(out=out[b * NODES : (b + 1) * NODES, :], in_=v[:])
+            nc.sync.dma_start(out=out[b * NODES : (b + 1) * NODES, :], in_=v[:])
 
         w_raw = const.tile([P, PACK, HID], BF16)
         bias = const.tile([P, HID], BF16)
+        w_rows = w_map.rearrange("(t p) n -> p t n", p=P)
+        for c in range(HID // N_TILE):
+            cols = slice(c * N_TILE, (c + 1) * N_TILE)
+            nc.sync.dma_start(out=w_raw[:, :, cols], in_=w_rows[:, :, cols])
         load_neigh(0)
         load_neigh(1)
-        nc.sync.dma_start(out=w_raw[:], in_=w_map.rearrange("(t p) n -> p t n", p=P))
         load_src(0)
         nc.sync.dma_start(out=bias[:], in_=b_map.partition_broadcast(P))
         for b in range(1, BATCH):
@@ -185,6 +189,16 @@ def tile_syntacticgcn_kernel(tc, src, neigh, w_map, b_map, out):
         w_grouped = const.tile([P, HID, PACK], BF16, align_bytes=64)
         w_codes = const.tile([P, HID], U32, align_bytes=64)
         w_scales = const.tile([P, HID], U8, align_bytes=64)
+        for c in range(HID // N_TILE):
+            cols = slice(c * N_TILE, (c + 1) * N_TILE)
+            nc.vector.tensor_copy(
+                out=w_grouped[:, cols, :], in_=w_raw[:, :, cols].rearrange("p t n -> p n t")
+            )
+        nc.vector.quantize_mx(
+            out=w_codes[:].bitcast(FP8X4),
+            scales=w_scales[:],
+            in_=w_grouped[:].rearrange("p n t -> p (n t)"),
+        )
 
         for m in range(BATCH + 2):
             folds = m < BATCH
@@ -195,31 +209,24 @@ def tile_syntacticgcn_kernel(tc, src, neigh, w_map, b_map, out):
             if folds:
                 count_slots(m)
                 halve_slots(m, 8)
+            if scales:
+                clamp_count(m - 1)
             if finishes:
                 quantise_and_multiply(m - 2)
             if scales:
                 sum_src(m - 1)
-                clamp_count(m - 1)
+                invert_count(m - 1)
             if folds:
                 halve_slots(m, 4)
+            if scales:
+                scale_and_transpose(m - 1)
             if finishes:
                 add_bias(m - 2, 0)
-            if scales:
-                invert_count(m - 1)
             if folds:
                 halve_slots(m, 2)
             if finishes:
                 add_bias(m - 2, 1)
-            if scales:
-                scale_and_transpose(m - 1)
             if folds:
                 halve_slots(m, 1)
             if finishes:
                 leaky_and_store(m - 2)
-            if m == 0:
-                nc.vector.tensor_copy(out=w_grouped[:], in_=w_raw[:].rearrange("p t n -> p n t"))
-                nc.vector.quantize_mx(
-                    out=w_codes[:].bitcast(FP8X4),
-                    scales=w_scales[:],
-                    in_=w_grouped[:].rearrange("p n t -> p (n t)"),
-                )

@@ -75,7 +75,7 @@ def tile_syntacticgcn_kernel(tc, src, neigh, w_map, b_map, out):
 
         def clamp_count(b):
             num_floor = work.tile([P, 1], F32)
-            nc.vector.tensor_scalar_max(out=num_floor[:], in0=nums[b][:], scalar1=1.0)
+            nc.gpsimd.tensor_scalar_max(out=num_floor[:], in0=nums[b][:], scalar1=1.0)
             nums[b] = num_floor
 
         def invert_count(b):
@@ -153,11 +153,13 @@ def tile_syntacticgcn_kernel(tc, src, neigh, w_map, b_map, out):
             )
 
         def leaky_and_store(b):
-            v = result_tiles[b]
-            nc.vector.scalar_tensor_tensor(
-                out=v[:], in0=v[:], scalar=SLOPE, in1=v[:], op0=ALU.mult, op1=ALU.max
-            )
-            nc.sync.dma_start(out=out[b * NODES : (b + 1) * NODES, :], in_=v[:])
+            for c in range(HID // N_TILE):
+                cols = slice(c * N_TILE, (c + 1) * N_TILE)
+                v = result_tiles[b][:, cols]
+                nc.vector.scalar_tensor_tensor(
+                    out=v, in0=v, scalar=SLOPE, in1=v, op0=ALU.mult, op1=ALU.max
+                )
+                nc.sync.dma_start(out=out[b * NODES : (b + 1) * NODES, cols], in_=v)
 
         w_raw = const.tile([P, PACK, HID], BF16)
         bias = const.tile([P, HID], BF16)
@@ -200,19 +202,22 @@ def tile_syntacticgcn_kernel(tc, src, neigh, w_map, b_map, out):
             in_=w_grouped[:].rearrange("p n t -> p (n t)"),
         )
 
-        for m in range(BATCH + 2):
+        for m in range(BATCH + 3):
             folds = m < BATCH
             scales = 1 <= m <= BATCH
-            finishes = m >= 2
-            if finishes:
+            multiplies = 2 <= m <= BATCH + 1
+            stores = m >= 3
+            if multiplies:
                 group_hidden(m - 2)
             if folds:
                 count_slots(m)
                 halve_slots(m, 8)
             if scales:
                 clamp_count(m - 1)
-            if finishes:
+            if multiplies:
                 quantise_and_multiply(m - 2)
+            if stores:
+                leaky_and_store(m - 3)
             if scales:
                 sum_src(m - 1)
                 invert_count(m - 1)
@@ -220,13 +225,11 @@ def tile_syntacticgcn_kernel(tc, src, neigh, w_map, b_map, out):
                 halve_slots(m, 4)
             if scales:
                 scale_and_transpose(m - 1)
-            if finishes:
+            if multiplies:
                 add_bias(m - 2, 0)
             if folds:
                 halve_slots(m, 2)
-            if finishes:
+            if multiplies:
                 add_bias(m - 2, 1)
             if folds:
                 halve_slots(m, 1)
-            if finishes:
-                leaky_and_store(m - 2)

@@ -87,7 +87,8 @@ def tile_syntacticgcn_kernel(tc, src, neigh, w_map, b_map, out):
             folded = partial.get(b, neigh_tiles[b])
             pool = work if width == 1 else scratch
             halved = pool.tile([P, width, FEAT], F32, name="sum%d" % width)
-            nc.vector.tensor_tensor(
+            engine = nc.gpsimd if width == 1 else nc.vector
+            engine.tensor_tensor(
                 out=halved[:],
                 in0=folded[:, 0:width, :],
                 in1=folded[:, width : 2 * width, :],
@@ -110,7 +111,14 @@ def tile_syntacticgcn_kernel(tc, src, neigh, w_map, b_map, out):
 
         def scale_and_transpose(b):
             mean = work.tile([P, FEAT], F32)
-            nc.vector.tensor_scalar_mul(out=mean[:], in0=partial[b][:, 0, :], scalar1=nums[b][:, 0:1])
+            nc.gpsimd.tensor_scalar(
+                out=mean[:],
+                in0=partial[b][:, 0, :],
+                scalar1=nums[b][:, 0:1],
+                scalar2=0.0,
+                op0=ALU.mult,
+                op1=ALU.add,
+            )
             for h in range(FEAT_HALVES):
                 nc.tensor.transpose(
                     hidden_banks[b][:, FEAT_HALVES + h, :], mean[:, h * P : (h + 1) * P], identity[:]

from contextlib import ExitStack

import concourse.mybir as mybir
from concourse.masks import make_identity

F32 = mybir.dt.float32
BF16 = mybir.dt.bfloat16
U32 = mybir.dt.uint32
U8 = mybir.dt.uint8
FP8X4 = mybir.dt.float8_e4m3fn_x4
ALU = mybir.AluOpType
ACT = mybir.ActivationFunctionType
AXIS = mybir.AxisListType

P = 128
PACK = 4
BATCH, NODES, SLOTS, FEAT, HID = 8, 128, 16, 256, 1024
GROUP_NODES = P // SLOTS
GROUPS = NODES // GROUP_NODES
FEAT_HALVES = FEAT // P
N_TILE = 512
SLOPE = 0.01

FLOPS = 2 * BATCH * NODES * 2 * FEAT * HID


def tile_syntacticgcn_kernel(tc, src, neigh, w_map, b_map, out):
    nc = tc.nc
    with ExitStack() as ctx:
        const = ctx.enter_context(tc.tile_pool(name="const", bufs=1))
        loads = ctx.enter_context(tc.tile_pool(name="loads", bufs=BATCH))
        results = ctx.enter_context(tc.tile_pool(name="results", bufs=BATCH))
        scratch = ctx.enter_context(tc.tile_pool(name="scratch", bufs=1))
        work = ctx.enter_context(tc.tile_pool(name="work", bufs=2))
        psum_hidden = ctx.enter_context(tc.psum_pool(name="psum_hidden", bufs=2))
        psum_out = ctx.enter_context(tc.psum_pool(name="psum_out", bufs=4))
        ctx.enter_context(tc.manual_schedule())

        src_tiles = {}
        neigh_tiles = {}
        partial = {}
        nums = {}
        hidden_banks = {}
        grouped_tiles = {}
        acc_banks = {}
        result_tiles = {}

        def load_neigh(b):
            neigh_t = loads.tile([P, SLOTS, FEAT], BF16)
            nc.sync.dma_start(out=neigh_t[:], in_=neigh[b])
            neigh_tiles[b] = neigh_t

        def load_src(b):
            src_t = loads.tile([P, GROUPS, FEAT], BF16)
            by_group = src[b].rearrange("(g j) s f -> (j s) g f", j=GROUP_NODES)
            for first in range(0, GROUPS, GROUPS // 2):
                groups = slice(first, first + GROUPS // 2)
                nc.sync.dma_start(out=src_t[:, groups, :], in_=by_group[:, groups, :])
            src_tiles[b] = src_t

        def count_slots(b):
            abs_values = scratch.tile([P, SLOTS, FEAT], BF16)
            abs_sum = work.tile([P, SLOTS], F32)
            for s in range(SLOTS):
                nc.scalar.activation(
                    out=abs_values[:, s, :],
                    in_=neigh_tiles[b][:, s, :],
                    func=ACT.Abs,
                    accum_out=abs_sum[:, s : s + 1],
                )
            valid = work.tile([P, SLOTS], F32)
            num = work.tile([P, 1], F32)
            nc.scalar.activation(out=valid[:], in_=abs_sum[:], func=ACT.Sign, accum_out=num[:])
            nums[b] = num

        def clamp_count(b):
            num_floor = work.tile([P, 1], F32)
            nc.gpsimd.tensor_scalar_max(out=num_floor[:], in0=nums[b][:], scalar1=1.0)
            nums[b] = num_floor

        def invert_count(b):
            inv_num = work.tile([P, 1], F32)
            nc.vector.reciprocal(out=inv_num[:], in_=nums[b][:])
            nums[b] = inv_num

        def halve_slots(b, width):
            folded = partial.get(b, neigh_tiles[b])
            pool = work if width == 1 else scratch
            halved = pool.tile([P, width, FEAT], F32, name="sum%d" % width)
            engine = nc.gpsimd if width == 1 else nc.vector
            engine.tensor_tensor(
                out=halved[:],
                in0=folded[:, 0:width, :],
                in1=folded[:, width : 2 * width, :],
                op=ALU.add,
            )
            partial[b] = halved

        def sum_src(b):
            hidden_t = psum_hidden.tile([P, PACK, NODES], F32)
            for g in range(GROUPS):
                for h in range(FEAT_HALVES):
                    nc.tensor.matmul(
                        out=hidden_t[:, h, g * GROUP_NODES : (g + 1) * GROUP_NODES],
                        lhsT=src_tiles[b][:, g, h * P : (h + 1) * P],
                        rhs=select[:],
                        start=True,
                        stop=True,
                    )
            hidden_banks[b] = hidden_t

        def scale_and_transpose(b):
            mean = work.tile([P, FEAT], F32)
            nc.gpsimd.tensor_scalar(
                out=mean[:],
                in0=partial[b][:, 0, :],
                scalar1=nums[b][:, 0:1],
                scalar2=0.0,
                op0=ALU.mult,
                op1=ALU.add,
            )
            for h in range(FEAT_HALVES):
                nc.tensor.transpose(
                    hidden_banks[b][:, FEAT_HALVES + h, :], mean[:, h * P : (h + 1) * P], identity[:]
                )

        def group_hidden(b):
            grouped = work.tile([P, NODES, PACK], BF16, align_bytes=64)
            nc.scalar.copy(out=grouped[:], in_=hidden_banks[b][:].rearrange("p t n -> p n t"))
            grouped_tiles[b] = grouped

        def quantise_and_multiply(b):
            h_codes = work.tile([P, NODES], U32, align_bytes=64)
            h_scales = work.tile([P, NODES], U8, align_bytes=64)
            nc.vector.quantize_mx(
                out=h_codes[:].bitcast(FP8X4),
                scales=h_scales[:],
                in_=grouped_tiles[b][:].rearrange("p n t -> p (n t)"),
            )
            for c in range(HID // N_TILE):
                cols = slice(c * N_TILE, (c + 1) * N_TILE)
                acc = psum_out.tile([P, N_TILE], F32)
                nc.tensor.matmul_mx(
                    out=acc[:],
                    lhsT=h_codes[:].bitcast(FP8X4),
                    lhsT_scale=h_scales[:],
                    rhs=w_codes[:, cols].bitcast(FP8X4),
                    rhs_scale=w_scales[:, cols],
                    start=True,
                    stop=True,
                )
                acc_banks[(b, c)] = acc

        def add_bias(b, c):
            if c == 0:
                result = results.tile([P, HID], F32)
                result_tiles[b] = result
            cols = slice(c * N_TILE, (c + 1) * N_TILE)
            nc.vector.tensor_tensor(
                out=result_tiles[b][:, cols], in0=acc_banks[(b, c)][:], in1=bias[:, cols], op=ALU.add
            )

        def leaky_and_store(b):
            for c in range(HID // N_TILE):
                cols = slice(c * N_TILE, (c + 1) * N_TILE)
                v = result_tiles[b][:, cols]
                nc.vector.scalar_tensor_tensor(
                    out=v, in0=v, scalar=SLOPE, in1=v, op0=ALU.mult, op1=ALU.max
                )
                nc.sync.dma_start(out=out[b * NODES : (b + 1) * NODES, cols], in_=v)

        w_raw = const.tile([P, PACK, HID], BF16)
        bias = const.tile([P, HID], BF16)
        w_rows = w_map.rearrange("(t p) n -> p t n", p=P)
        for c in range(HID // N_TILE):
            cols = slice(c * N_TILE, (c + 1) * N_TILE)
            nc.sync.dma_start(out=w_raw[:, :, cols], in_=w_rows[:, :, cols])
        load_neigh(0)
        load_neigh(1)
        load_src(0)
        nc.sync.dma_start(out=bias[:], in_=b_map.partition_broadcast(P))
        for b in range(1, BATCH):
            if b + 1 < BATCH:
                load_neigh(b + 1)
            load_src(b)

        identity = const.tile([P, P], F32)
        make_identity(nc, identity[:])
        select_f32 = const.tile([P, GROUP_NODES], F32)
        nc.vector.tensor_reduce(
            out=select_f32[:],
            in_=identity[:].rearrange("p (j s) -> p j s", s=SLOTS),
            axis=AXIS.X,
            op=ALU.add,
        )
        select = const.tile([P, GROUP_NODES], BF16)
        nc.vector.tensor_copy(out=select[:], in_=select_f32[:])

        w_grouped = const.tile([P, HID, PACK], BF16, align_bytes=64)
        w_codes = const.tile([P, HID], U32, align_bytes=64)
        w_scales = const.tile([P, HID], U8, align_bytes=64)
        for c in range(HID // N_TILE):
            cols = slice(c * N_TILE, (c + 1) * N_TILE)
            nc.vector.tensor_copy(
                out=w_grouped[:, cols, :], in_=w_raw[:, :, cols].rearrange("p t n -> p n t")
            )
        nc.vector.quantize_mx(
            out=w_codes[:].bitcast(FP8X4),
            scales=w_scales[:],
            in_=w_grouped[:].rearrange("p n t -> p (n t)"),
        )

        for m in range(BATCH + 3):
            folds = m < BATCH
            scales = 1 <= m <= BATCH
            multiplies = 2 <= m <= BATCH + 1
            stores = m >= 3
            if multiplies:
                group_hidden(m - 2)
            if folds:
                count_slots(m)
                halve_slots(m, 8)
            if scales:
                clamp_count(m - 1)
            if multiplies:
                quantise_and_multiply(m - 2)
            if stores:
                leaky_and_store(m - 3)
            if scales:
                sum_src(m - 1)
                invert_count(m - 1)
            if folds:
                halve_slots(m, 4)
            if scales:
                scale_and_transpose(m - 1)
            if multiplies:
                add_bias(m - 2, 0)
            if folds:
                halve_slots(m, 2)
            if multiplies:
                add_bias(m - 2, 1)
            if folds:
                halve_slots(m, 1)
